import numpy as np
import ml_dtypes


BF16 = ml_dtypes.bfloat16


def bf(x):
    return np.asarray(x, np.float32).astype(BF16)


def f64(x):
    return np.asarray(x).astype(np.float64)


E2M1 = np.array([0.0, 0.5, 1.0, 1.5, 2.0, 3.0, 4.0, 6.0, -0.0, -0.5, -1.0, -1.5, -2.0, -3.0, -4.0, -6.0])


def pack_weight(w, fmt):
    k, n = w.shape
    w = f64(bf(w)).reshape(k // 32, 32, n)
    amax = np.abs(w).max(1)
    if fmt == "e4m3":
        byte = np.frexp(amax)[1] - 1 + 127 - 7
    else:
        mant, ex = np.frexp(amax / 6.0)
        byte = np.where(mant > 0.5, ex, ex - 1) + 127
    byte = np.clip(np.where(amax > 0, byte, 1), 1, 254)
    scaled = (w * np.exp2(127.0 - byte)[:, None, :]).reshape(k, n).astype(np.float32)
    by_word = np.ascontiguousarray(scaled.reshape(k // 512, 128, 4, n).transpose(0, 1, 3, 2))
    if fmt == "e4m3":
        words = by_word.astype(ml_dtypes.float8_e4m3fn).view(np.uint8)
    else:
        c = by_word.astype(ml_dtypes.float4_e2m1fn).view(np.uint8) & 0xF
        words = c[..., 0::2] | (c[..., 1::2] << 4)
    return np.ascontiguousarray(words), np.ascontiguousarray(byte.astype(np.uint8).reshape(k // 512, 16, n))


def unpack_weight(words, scales, fmt):
    g, p, n, _ = words.shape
    if fmt == "e4m3":
        vals = np.ascontiguousarray(words).view(ml_dtypes.float8_e4m3fn).astype(np.float64)
    else:
        nib = np.empty((g, p, n, 4), np.uint8)
        nib[..., 0::2] = words & 0xF
        nib[..., 1::2] = words >> 4
        vals = E2M1[nib]
    vals = vals * np.repeat(np.exp2(scales.astype(np.float64) - 127.0), 8, axis=1)[..., None]
    return vals.transpose(0, 1, 3, 2).reshape(g * 512, n)

def pack4(w):
    words, scales = pack_weight(w, "e2m1")
    return words.reshape(words.shape[0], 128, -1), scales


def unpack4(words, scales):
    return unpack_weight(words.reshape(words.shape[0], 128, -1, 2), scales, "e2m1")


def kspread(k):
    return np.exp2(np.repeat(np.random.randint(-6, 7, k // 32), 32).astype(np.float64))


B, T, C, H, KV, HD = 4, 1024, 2048, 16, 4, 128
NQ = H * HD
NK = KV * HD
HALF = HD // 2
ROPE_THETA = 10000.0


def apply_rope(u, cos, sin):
    ur = u.reshape(*u.shape[:-1], HALF, 2)
    ue, uo = ur[..., 0], ur[..., 1]
    c = cos[None, :, None, :]
    s = sin[None, :, None, :]
    out_e = ue * c - uo * s
    out_o = ue * s + uo * c
    return np.stack([out_e, out_o], axis=-1).reshape(u.shape)


def setup_inputs():
    s = kspread(C)
    inv_freq = 1.0 / ROPE_THETA ** (np.arange(0, HD, 2) / HD)
    angles = np.arange(T)[:, None] * inv_freq[None, :]
    x = np.random.standard_normal((B, T, C)) * s
    x_words, x_scales = pack4(np.ascontiguousarray(x.reshape(B * T, C).T))
    w = np.random.standard_normal((NQ + NK + NK, C)) / np.sqrt(C) / s[None, :]
    words, scales = pack4(np.ascontiguousarray(w.T))
    return {"x_words": x_words,
            "x_scales": x_scales,
            "w_qkv_words": words,
            "w_qkv_scales": scales,
            "freqs_cos": bf(np.cos(angles)),
            "freqs_sin": bf(np.sin(angles))}


def reference(x_words, x_scales, w_qkv_words, w_qkv_scales, freqs_cos, freqs_sin):
    cos, sin = f64(freqs_cos), f64(freqs_sin)
    xq = unpack4(x_words, x_scales).T.reshape(B, T, C)
    qkv = xq @ unpack4(w_qkv_words, w_qkv_scales)
    q = qkv[..., :NQ].reshape(B, T, H, HD)
    k = qkv[..., NQ:NQ + NK].reshape(B, T, KV, HD)
    v = qkv[..., NQ + NK:].reshape(B, T, KV, HD)
    return apply_rope(q, cos, sin), apply_rope(k, cos, sin), v

@@ -1,0 +1,157 @@
+from contextlib import ExitStack
+
+import concourse.mybir as mybir
+
+FLOPS = 2 * 4096 * 2048 * 3072
+
+F32 = mybir.dt.float32
+BF16 = mybir.dt.bfloat16
+I32 = mybir.dt.int32
+U8 = mybir.dt.uint8
+FP4X4 = mybir.dt.float4_e2m1fn_x4
+MULT = mybir.AluOpType.mult
+ADD = mybir.AluOpType.add
+
+P = 128
+PASSES = 4
+TOK_TILE = 128
+N_BLK = 512
+TILES_PER_CHUNK = 4
+CHUNK = TOK_TILE * TILES_PER_CHUNK
+N_CHUNKS = 4096 // CHUNK
+N_BLOCKS = 3072 // N_BLK
+POS_TILES = 1024 // TOK_TILE
+HEADS_PER_BLK = N_BLK // 128
+
+
+def load_codes(nc, tile_ap, words, col0, ncols):
+    nc.sync.dma_start(
+        out=tile_ap.bitcast(I32),
+        in_=words[:, :, 2 * col0 : 2 * (col0 + ncols)].rearrange("g p b -> p g b").bitcast(I32),
+    )
+
+
+def load_scales(nc, plane, scales, col0, ncols):
+    for q in range(4):
+        nc.sync.dma_start(
+            out=plane[32 * q : 32 * q + 4, :, :].bitcast(I32),
+            in_=scales[:, 4 * q : 4 * q + 4, col0 : col0 + ncols].rearrange("g r n -> r g n").bitcast(I32),
+        )
+
+
+def tile_causalselfattention_pa_kernel(
+    tc, x_words, x_scales, w_qkv_words, w_qkv_scales, freqs_cos, freqs_sin, out_0, out_1, out_2
+):
+    nc = tc.nc
+    q_rows = out_0.rearrange("b t h d -> (b t) (h d)")
+    k_rows = out_1.rearrange("b t h d -> (b t) (h d)")
+    v_rows = out_2.rearrange("b t h d -> (b t) (h d)")
+
+    with ExitStack() as ctx:
+        keep = ctx.enter_context(tc.tile_pool(name="keep", bufs=1))
+        prod = ctx.enter_context(tc.tile_pool(name="prod", bufs=5))
+        cross = ctx.enter_context(tc.tile_pool(name="cross", bufs=3))
+        vals = ctx.enter_context(tc.tile_pool(name="vals", bufs=3))
+        psum = ctx.enter_context(tc.psum_pool(name="psum", bufs=8))
+        ctx.enter_context(tc.manual_schedule())
+
+        xc = [keep.tile([P, PASSES, 2 * CHUNK], U8, name="xc%d" % s, align_bytes=64) for s in range(N_CHUNKS)]
+        xs = [keep.tile([P, PASSES, CHUNK], U8, name="xs%d" % s, align_bytes=64) for s in range(N_CHUNKS)]
+        wc = [keep.tile([P, PASSES, 2 * N_BLK], U8, name="wc%d" % n, align_bytes=64) for n in range(N_BLOCKS)]
+        ws = [keep.tile([P, PASSES, N_BLK], U8, name="ws%d" % n, align_bytes=64) for n in range(N_BLOCKS)]
+        cos_raw = keep.tile([P, POS_TILES, 64], BF16, name="cos_raw")
+        sin_pm = keep.tile([P, 2, POS_TILES, 64], BF16, name="sin_pm")
+        cos2 = keep.tile([P, POS_TILES, 128], F32, name="cos2")
+        sin2 = keep.tile([P, POS_TILES, 128], F32, name="sin2")
+
+        first_blk = N_BLOCKS - 1
+        nc.vector.memset(xs[0][:].bitcast(I32), 0)
+        nc.vector.memset(ws[first_blk][:].bitcast(I32), 0)
+        load_codes(nc, wc[first_blk][:], w_qkv_words, first_blk * N_BLK, N_BLK)
+        load_codes(nc, xc[0][:], x_words, 0, CHUNK)
+        load_scales(nc, xs[0], x_scales, 0, CHUNK)
+        load_scales(nc, ws[first_blk], w_qkv_scales, first_blk * N_BLK, N_BLK)
+        for n in range(N_BLOCKS - 1):
+            nc.vector.memset(ws[n][:].bitcast(I32), 0)
+            load_codes(nc, wc[n][:], w_qkv_words, n * N_BLK, N_BLK)
+            load_scales(nc, ws[n], w_qkv_scales, n * N_BLK, N_BLK)
+            if n == 0:
+                nc.sync.dma_start(out=cos_raw[:], in_=freqs_cos.rearrange("(a p) j -> p a j", p=P))
+                nc.sync.dma_start(out=sin_pm[:, 1], in_=freqs_sin.rearrange("(a p) j -> p a j", p=P))
+        for s in range(1, N_CHUNKS):
+            nc.vector.memset(xs[s][:].bitcast(I32), 0)
+            load_codes(nc, xc[s][:], x_words, s * CHUNK, CHUNK)
+            load_scales(nc, xs[s], x_scales, s * CHUNK, CHUNK)
+
+        nc.gpsimd.tensor_scalar(
+            out=cos2[:].rearrange("p a (j t) -> p a j t", t=2),
+            in0=cos_raw[:].unsqueeze(3).to_broadcast([P, POS_TILES, 64, 2]),
+            scalar1=1.0,
+            scalar2=0.0,
+            op0=MULT,
+            op1=ADD,
+        )
+        nc.vector.tensor_scalar_mul(out=sin_pm[:, 0], in0=sin_pm[:, 1], scalar1=-1.0)
+        nc.vector.tensor_copy(
+            out=sin2[:].rearrange("p a (j t) -> p a j t", t=2),
+            in_=sin_pm[:].rearrange("p t a j -> p a j t"),
+        )
+
+        for s in range(N_CHUNKS):
+            last = s == N_CHUNKS - 1
+            order = list(range(N_BLOCKS))
+            if s == 0:
+                order = [first_blk] + order[:-1]
+            for n in order:
+                rope = n < N_BLOCKS - 1
+                if n < 4:
+                    dst = q_rows[s * CHUNK : (s + 1) * CHUNK, n * N_BLK : (n + 1) * N_BLK]
+                elif n == 4:
+                    dst = k_rows[s * CHUNK : (s + 1) * CHUNK, :]
+                else:
+                    dst = v_rows[s * CHUNK : (s + 1) * CHUNK, :]
+                dst = dst.rearrange("(i p) c -> p i c", p=P)
+                if rope:
+                    direct = prod.tile([P, TILES_PER_CHUNK, N_BLK], F32, name="direct")
+                    crossed = cross.tile([P, TILES_PER_CHUNK, N_BLK], F32, name="crossed")
+                else:
+                    direct = vals.tile([P, TILES_PER_CHUNK, N_BLK], F32, name="value")
+                for i in range(TILES_PER_CHUNK):
+                    acc = psum.tile([P, N_BLK], F32, name="acc")
+                    for g in range(PASSES):
+                        nc.tensor.matmul_mx(
+                            out=acc[:],
+                            lhsT=xc[s][:, g, 2 * TOK_TILE * i : 2 * TOK_TILE * (i + 1)].bitcast(FP4X4),
+                            lhsT_scale=xs[s][:, g, TOK_TILE * i : TOK_TILE * (i + 1)],
+                            rhs=wc[n][:, g, :].bitcast(FP4X4),
+                            rhs_scale=ws[n][:, g, :],
+                            start=(g == 0),
+                            stop=(g == PASSES - 1),
+                        )
+                    if rope:
+                        a = (s * TILES_PER_CHUNK + i) % POS_TILES
+                        nc.vector.tensor_tensor(
+                            out=direct[:, i, :].rearrange("p (h d) -> p h d", h=HEADS_PER_BLK),
+                            in0=acc[:].rearrange("p (h d) -> p h d", h=HEADS_PER_BLK),
+                            in1=cos2[:, a, :].unsqueeze(1).to_broadcast([P, HEADS_PER_BLK, 128]),
+                            op=MULT,
+                        )
+                        nc.vector.tensor_tensor(
+                            out=crossed[:, i, :].rearrange("p (h j t) -> p h j t", h=HEADS_PER_BLK, t=2),
+                            in0=acc[:].rearrange("p (h j t) -> p h j t", h=HEADS_PER_BLK, t=2)[:, :, :, ::-1],
+                            in1=sin2[:, a, :].rearrange("p (j t) -> p j t", t=2).unsqueeze(1).to_broadcast([P, HEADS_PER_BLK, 64, 2]),
+                            op=MULT,
+                        )
+                    else:
+                        nc.scalar.copy(out=direct[:, i, :], in_=acc[:])
+                        if last:
+                            nc.scalar.dma_start(out=dst[:, i, :], in_=direct[:, i, :])
+                if rope and last and n == 4:
+                    for i in range(TILES_PER_CHUNK):
+                        nc.vector.tensor_tensor(out=direct[:, i, :], in0=direct[:, i, :], in1=crossed[:, i, :], op=ADD)
+                        nc.sync.dma_start(out=dst[:, i, :], in_=direct[:, i, :])
+                elif rope:
+                    nc.gpsimd.tensor_tensor(out=direct[:], in0=direct[:], in1=crossed[:], op=ADD)
+                    nc.sync.dma_start(out=dst, in_=direct[:])
+                elif not last:
+                    nc.scalar.dma_start(out=dst, in_=direct[:])

@@ -22,6 +22,7 @@ N_CHUNKS = 4096 // CHUNK
 N_BLOCKS = 3072 // N_BLK
 POS_TILES = 1024 // TOK_TILE
 HEADS_PER_BLK = N_BLK // 128
+N_WARM = 10
 
 
 def load_codes(nc, tile_ap, words, col0, ncols):
@@ -31,8 +32,8 @@ def load_codes(nc, tile_ap, words, col0, ncols):
     )
 
 
-def load_scales(nc, plane, scales, col0, ncols):
-    for q in range(4):
+def load_scales(nc, plane, scales, col0, ncols, quadrants=(0, 1, 2, 3)):
+    for q in quadrants:
         nc.sync.dma_start(
             out=plane[32 * q : 32 * q + 4, :, :].bitcast(I32),
             in_=scales[:, 4 * q : 4 * q + 4, col0 : col0 + ncols].rearrange("g r n -> r g n").bitcast(I32),
@@ -63,14 +64,20 @@ def tile_causalselfattention_pa_kernel(
         sin_pm = keep.tile([P, 2, POS_TILES, 64], BF16, name="sin_pm")
         cos2 = keep.tile([P, POS_TILES, 128], F32, name="cos2")
         sin2 = keep.tile([P, POS_TILES, 128], F32, name="sin2")
+        warm = keep.tile([P, P + N_BLK], BF16, name="warm")
 
         first_blk = N_BLOCKS - 1
-        nc.vector.memset(xs[0][:].bitcast(I32), 0)
+        nc.gpsimd.memset(xs[0][:].bitcast(F32), 0.0)
+        nc.vector.memset(warm[:], 0.0)
         nc.vector.memset(ws[first_blk][:].bitcast(I32), 0)
+        load_scales(nc, xs[0], x_scales, 0, CHUNK, (0, 1))
         load_codes(nc, wc[first_blk][:], w_qkv_words, first_blk * N_BLK, N_BLK)
         load_codes(nc, xc[0][:], x_words, 0, CHUNK)
-        load_scales(nc, xs[0], x_scales, 0, CHUNK)
+        load_scales(nc, xs[0], x_scales, 0, CHUNK, (2, 3))
         load_scales(nc, ws[first_blk], w_qkv_scales, first_blk * N_BLK, N_BLK)
+        warm_acc = psum.tile([P, N_BLK], F32, name="acc")
+        for w in range(N_WARM):
+            nc.tensor.matmul(out=warm_acc[:], lhsT=warm[:, 0:P], rhs=warm[:, P : P + N_BLK], start=True, stop=True)
         for n in range(N_BLOCKS - 1):
             nc.vector.memset(ws[n][:].bitcast(I32), 0)
             load_codes(nc, wc[n][:], w_qkv_words, n * N_BLK, N_BLK)
@@ -142,6 +149,10 @@ def tile_causalselfattention_pa_kernel(
                             in1=sin2[:, a, :].rearrange("p (j t) -> p j t", t=2).unsqueeze(1).to_broadcast([P, HEADS_PER_BLK, 64, 2]),
                             op=MULT,
                         )
+                        if last and n < 4 and i % 2 == 1:
+                            half = slice(i - 1, i + 1)
+                            nc.gpsimd.tensor_tensor(out=direct[:, half, :], in0=direct[:, half, :], in1=crossed[:, half, :], op=ADD)
+                            nc.sync.dma_start(out=dst[:, half, :], in_=direct[:, half, :])
                     else:
                         nc.scalar.copy(out=direct[:, i, :], in_=acc[:])
                         if last:
@@ -150,7 +161,7 @@ def tile_causalselfattention_pa_kernel(
                     for i in range(TILES_PER_CHUNK):
                         nc.vector.tensor_tensor(out=direct[:, i, :], in0=direct[:, i, :], in1=crossed[:, i, :], op=ADD)
                         nc.sync.dma_start(out=dst[:, i, :], in_=direct[:, i, :])
-                elif rope:
+                elif rope and not last:
                     nc.gpsimd.tensor_tensor(out=direct[:], in0=direct[:], in1=crossed[:], op=ADD)
                     nc.sync.dma_start(out=dst, in_=direct[:])
                 elif not last:

@@ -22,7 +22,7 @@ N_CHUNKS = 4096 // CHUNK
 N_BLOCKS = 3072 // N_BLK
 POS_TILES = 1024 // TOK_TILE
 HEADS_PER_BLK = N_BLK // 128
-N_WARM = 10
+N_WARM = 13
 
 
 def load_codes(nc, tile_ap, words, col0, ncols):
@@ -32,11 +32,11 @@ def load_codes(nc, tile_ap, words, col0, ncols):
     )
 
 
-def load_scales(nc, plane, scales, col0, ncols, quadrants=(0, 1, 2, 3)):
-    for q in quadrants:
+def load_scales(nc, plane, scales, col0, ncols, rows=(0, 1, 2, 3)):
+    for r in rows:
         nc.sync.dma_start(
-            out=plane[32 * q : 32 * q + 4, :, :].bitcast(I32),
-            in_=scales[:, 4 * q : 4 * q + 4, col0 : col0 + ncols].rearrange("g r n -> r g n").bitcast(I32),
+            out=plane[r : P : 32, :, :].bitcast(I32),
+            in_=scales[:, r : 16 : 4, col0 : col0 + ncols].rearrange("g q n -> q g n").bitcast(I32),
         )
 
 
@@ -50,7 +50,7 @@ def tile_causalselfattention_pa_kernel(
 
     with ExitStack() as ctx:
         keep = ctx.enter_context(tc.tile_pool(name="keep", bufs=1))
-        prod = ctx.enter_context(tc.tile_pool(name="prod", bufs=5))
+        prod = ctx.enter_context(tc.tile_pool(name="prod", bufs=8))
         cross = ctx.enter_context(tc.tile_pool(name="cross", bufs=3))
         vals = ctx.enter_context(tc.tile_pool(name="vals", bufs=3))
         psum = ctx.enter_context(tc.psum_pool(name="psum", bufs=8))
@@ -87,8 +87,8 @@ def tile_causalselfattention_pa_kernel(
                 nc.sync.dma_start(out=sin_pm[:, 1], in_=freqs_sin.rearrange("(a p) j -> p a j", p=P))
         for s in range(1, N_CHUNKS):
             nc.vector.memset(xs[s][:].bitcast(I32), 0)
-            load_codes(nc, xc[s][:], x_words, s * CHUNK, CHUNK)
-            load_scales(nc, xs[s], x_scales, s * CHUNK, CHUNK)
+        load_codes(nc, xc[1][:], x_words, CHUNK, CHUNK)
+        load_scales(nc, xs[1], x_scales, CHUNK, CHUNK)
 
         nc.gpsimd.tensor_scalar(
             out=cos2[:].rearrange("p a (j t) -> p a j t", t=2),
@@ -110,6 +110,9 @@ def tile_causalselfattention_pa_kernel(
             if s == 0:
                 order = [first_blk] + order[:-1]
             for n in order:
+                if n == order[3] and s + 2 < N_CHUNKS:
+                    load_codes(nc, xc[s + 2][:], x_words, (s + 2) * CHUNK, CHUNK)
+                    load_scales(nc, xs[s + 2], x_scales, (s + 2) * CHUNK, CHUNK)
                 rope = n < N_BLOCKS - 1
                 if n < 4:
                     dst = q_rows[s * CHUNK : (s + 1) * CHUNK, n * N_BLK : (n + 1) * N_BLK]

@@ -22,13 +22,13 @@ N_CHUNKS = 4096 // CHUNK
 N_BLOCKS = 3072 // N_BLK
 POS_TILES = 1024 // TOK_TILE
 HEADS_PER_BLK = N_BLK // 128
-N_WARM = 13
+N_WARM = 6
 
 
-def load_codes(nc, tile_ap, words, col0, ncols):
+def load_codes(nc, tile_ap, words, col0, ncols, g0=0, g1=PASSES):
     nc.sync.dma_start(
         out=tile_ap.bitcast(I32),
-        in_=words[:, :, 2 * col0 : 2 * (col0 + ncols)].rearrange("g p b -> p g b").bitcast(I32),
+        in_=words[g0:g1, :, 2 * col0 : 2 * (col0 + ncols)].rearrange("g p b -> p g b").bitcast(I32),
     )
 
 
@@ -38,6 +38,18 @@ def load_scales(nc, plane, scales, col0, ncols, rows=(0, 1, 2, 3)):
             out=plane[r : P : 32, :, :].bitcast(I32),
             in_=scales[:, r : 16 : 4, col0 : col0 + ncols].rearrange("g q n -> q g n").bitcast(I32),
         )
+
+
+def load_scales_one_pass(nc, plane, scales, col0, ncols, g):
+    rows = scales.rearrange("g q n -> (g q) n")
+    words = ncols // 4
+    if g < PASSES - 1:
+        part = rows[16 * g : 16 * g + 28, col0 : col0 + ncols].bitcast(I32)
+        nc.sync.dma_start(out=plane[0:112, g, :].bitcast(I32), in_=part.unsqueeze(0).to_broadcast([4, 28, words]))
+    else:
+        part = rows[16 * g - 12 : 16 * g + 16, col0 : col0 + ncols].bitcast(I32)
+        nc.sync.dma_start(out=plane[16:128, g, :].bitcast(I32), in_=part.unsqueeze(0).to_broadcast([4, 28, words]))
+        nc.sync.dma_start(out=plane[0:16, g, :].bitcast(I32), in_=rows[16 * g : 16 * g + 16, col0 : col0 + ncols].bitcast(I32))
 
 
 def tile_causalselfattention_pa_kernel(
@@ -67,14 +79,19 @@ def tile_causalselfattention_pa_kernel(
         warm = keep.tile([P, P + N_BLK], BF16, name="warm")
 
         first_blk = N_BLOCKS - 1
-        nc.gpsimd.memset(xs[0][:].bitcast(F32), 0.0)
-        nc.vector.memset(warm[:], 0.0)
-        nc.vector.memset(ws[first_blk][:].bitcast(I32), 0)
-        load_scales(nc, xs[0], x_scales, 0, CHUNK, (0, 1))
-        load_codes(nc, wc[first_blk][:], w_qkv_words, first_blk * N_BLK, N_BLK)
-        load_codes(nc, xc[0][:], x_words, 0, CHUNK)
-        load_scales(nc, xs[0], x_scales, 0, CHUNK, (2, 3))
-        load_scales(nc, ws[first_blk], w_qkv_scales, first_blk * N_BLK, N_BLK)
+        nc.gpsimd.memset(warm[:], 0.0)
+        nc.vector.memset(xs[0][:].bitcast(I32), 0)
+        nc.vector.memset(ws[first_blk][:, 0:1, :].bitcast(I32), 0)
+        nc.vector.memset(ws[first_blk][:, 1:PASSES, :].bitcast(I32), 0)
+        load_codes(nc, wc[first_blk][:, 0:2, :], w_qkv_words, first_blk * N_BLK, N_BLK, 0, 2)
+        load_codes(nc, xc[0][:, 0:2, :], x_words, 0, CHUNK, 0, 2)
+        load_scales(nc, xs[0], x_scales, 0, CHUNK)
+        load_scales_one_pass(nc, ws[first_blk], w_qkv_scales, first_blk * N_BLK, N_BLK, 0)
+        load_scales_one_pass(nc, ws[first_blk], w_qkv_scales, first_blk * N_BLK, N_BLK, 1)
+        load_codes(nc, wc[first_blk][:, 2:4, :], w_qkv_words, first_blk * N_BLK, N_BLK, 2, 4)
+        load_codes(nc, xc[0][:, 2:4, :], x_words, 0, CHUNK, 2, 4)
+        load_scales_one_pass(nc, ws[first_blk], w_qkv_scales, first_blk * N_BLK, N_BLK, 2)
+        load_scales_one_pass(nc, ws[first_blk], w_qkv_scales, first_blk * N_BLK, N_BLK, 3)
         warm_acc = psum.tile([P, N_BLK], F32, name="acc")
         for w in range(N_WARM):
             nc.tensor.matmul(out=warm_acc[:], lhsT=warm[:, 0:P], rhs=warm[:, P : P + N_BLK], start=True, stop=True)
@@ -126,9 +143,28 @@ def tile_causalselfattention_pa_kernel(
                     crossed = cross.tile([P, TILES_PER_CHUNK, N_BLK], F32, name="crossed")
                 else:
                     direct = vals.tile([P, TILES_PER_CHUNK, N_BLK], F32, name="value")
-                for i in range(TILES_PER_CHUNK):
-                    acc = psum.tile([P, N_BLK], F32, name="acc")
+                accs = []
+                if s == 0 and n == first_blk:
+                    for i in range(TILES_PER_CHUNK):
+                        acc = psum.tile([P, N_BLK], F32, name="acc")
+                        accs.append(acc)
                     for g in range(PASSES):
+                        for i in range(TILES_PER_CHUNK):
+                            nc.tensor.matmul_mx(
+                                out=accs[i][:],
+                                lhsT=xc[s][:, g, 2 * TOK_TILE * i : 2 * TOK_TILE * (i + 1)].bitcast(FP4X4),
+                                lhsT_scale=xs[s][:, g, TOK_TILE * i : TOK_TILE * (i + 1)],
+                                rhs=wc[n][:, g, :].bitcast(FP4X4),
+                                rhs_scale=ws[n][:, g, :],
+                                start=(g == 0),
+                                stop=(g == PASSES - 1),
+                            )
+                for i in range(TILES_PER_CHUNK):
+                    if accs:
+                        acc = accs[i]
+                    else:
+                        acc = psum.tile([P, N_BLK], F32, name="acc")
+                    for g in range(PASSES if not accs else 0):
                         nc.tensor.matmul_mx(
                             out=acc[:],
                             lhsT=xc[s][:, g, 2 * TOK_TILE * i : 2 * TOK_TILE * (i + 1)].bitcast(FP4X4),

@@ -20,20 +20,23 @@ TILES_PER_CHUNK = 4
 CHUNK = TOK_TILE * TILES_PER_CHUNK
 N_CHUNKS = 4096 // CHUNK
 N_BLOCKS = 3072 // N_BLK
+V_BLK = N_BLOCKS - 1
+K_BLK = N_BLOCKS - 2
 POS_TILES = 1024 // TOK_TILE
 HEADS_PER_BLK = N_BLK // 128
 N_WARM = 6
+PERIOD = 28
 
 
-def load_codes(nc, tile_ap, words, col0, ncols, g0=0, g1=PASSES):
+def load_codes(nc, tile, words, col0, ncols, g0=0, g1=PASSES):
     nc.sync.dma_start(
-        out=tile_ap.bitcast(I32),
+        out=tile[:, g0:g1, :].bitcast(I32),
         in_=words[g0:g1, :, 2 * col0 : 2 * (col0 + ncols)].rearrange("g p b -> p g b").bitcast(I32),
     )
 
 
-def load_scales(nc, plane, scales, col0, ncols, rows=(0, 1, 2, 3)):
-    for r in rows:
+def load_scales(nc, plane, scales, col0, ncols):
+    for r in range(4):
         nc.sync.dma_start(
             out=plane[r : P : 32, :, :].bitcast(I32),
             in_=scales[:, r : 16 : 4, col0 : col0 + ncols].rearrange("g q n -> q g n").bitcast(I32),
@@ -42,13 +45,13 @@ def load_scales(nc, plane, scales, col0, ncols, rows=(0, 1, 2, 3)):
 
 def load_scales_one_pass(nc, plane, scales, col0, ncols, g):
     rows = scales.rearrange("g q n -> (g q) n")
-    words = ncols // 4
+    repeats = [4, PERIOD, ncols // 4]
     if g < PASSES - 1:
-        part = rows[16 * g : 16 * g + 28, col0 : col0 + ncols].bitcast(I32)
-        nc.sync.dma_start(out=plane[0:112, g, :].bitcast(I32), in_=part.unsqueeze(0).to_broadcast([4, 28, words]))
+        part = rows[16 * g : 16 * g + PERIOD, col0 : col0 + ncols].bitcast(I32)
+        nc.sync.dma_start(out=plane[0 : 4 * PERIOD, g, :].bitcast(I32), in_=part.unsqueeze(0).to_broadcast(repeats))
     else:
-        part = rows[16 * g - 12 : 16 * g + 16, col0 : col0 + ncols].bitcast(I32)
-        nc.sync.dma_start(out=plane[16:128, g, :].bitcast(I32), in_=part.unsqueeze(0).to_broadcast([4, 28, words]))
+        part = rows[16 * g + 16 - PERIOD : 16 * g + 16, col0 : col0 + ncols].bitcast(I32)
+        nc.sync.dma_start(out=plane[16:P, g, :].bitcast(I32), in_=part.unsqueeze(0).to_broadcast(repeats))
         nc.sync.dma_start(out=plane[0:16, g, :].bitcast(I32), in_=rows[16 * g : 16 * g + 16, col0 : col0 + ncols].bitcast(I32))
 
 
@@ -68,43 +71,68 @@ def tile_causalselfattention_pa_kernel(
         psum = ctx.enter_context(tc.psum_pool(name="psum", bufs=8))
         ctx.enter_context(tc.manual_schedule())
 
-        xc = [keep.tile([P, PASSES, 2 * CHUNK], U8, name="xc%d" % s, align_bytes=64) for s in range(N_CHUNKS)]
-        xs = [keep.tile([P, PASSES, CHUNK], U8, name="xs%d" % s, align_bytes=64) for s in range(N_CHUNKS)]
-        wc = [keep.tile([P, PASSES, 2 * N_BLK], U8, name="wc%d" % n, align_bytes=64) for n in range(N_BLOCKS)]
-        ws = [keep.tile([P, PASSES, N_BLK], U8, name="ws%d" % n, align_bytes=64) for n in range(N_BLOCKS)]
+        xc = [keep.tile([P, PASSES, 2 * CHUNK], U8, name="xc%d" % s, align_bytes=256) for s in range(N_CHUNKS)]
+        xs = [keep.tile([P, PASSES, CHUNK], U8, name="xs%d" % s, align_bytes=256) for s in range(N_CHUNKS)]
+        wc = [keep.tile([P, PASSES, 2 * N_BLK], U8, name="wc%d" % n, align_bytes=256) for n in range(N_BLOCKS)]
+        ws = [keep.tile([P, PASSES, N_BLK], U8, name="ws%d" % n, align_bytes=256) for n in range(N_BLOCKS)]
         cos_raw = keep.tile([P, POS_TILES, 64], BF16, name="cos_raw")
         sin_pm = keep.tile([P, 2, POS_TILES, 64], BF16, name="sin_pm")
         cos2 = keep.tile([P, POS_TILES, 128], F32, name="cos2")
         sin2 = keep.tile([P, POS_TILES, 128], F32, name="sin2")
         warm = keep.tile([P, P + N_BLK], BF16, name="warm")
 
-        first_blk = N_BLOCKS - 1
+        def mx_pass(acc, s, i, n, g, c0=0, c1=N_BLK):
+            nc.tensor.matmul_mx(
+                out=acc[:],
+                lhsT=xc[s][:, g, 2 * TOK_TILE * i : 2 * TOK_TILE * (i + 1)].bitcast(FP4X4),
+                lhsT_scale=xs[s][:, g, TOK_TILE * i : TOK_TILE * (i + 1)],
+                rhs=wc[n][:, g, 2 * c0 : 2 * c1].bitcast(FP4X4),
+                rhs_scale=ws[n][:, g, c0:c1],
+                start=(g == 0),
+                stop=(g == PASSES - 1),
+            )
+
+        def products(acc, direct, crossed, s, i):
+            a = (s * TILES_PER_CHUNK + i) % POS_TILES
+            nc.vector.tensor_tensor(
+                out=direct[:, i, :].rearrange("p (h d) -> p h d", h=HEADS_PER_BLK),
+                in0=acc[:].rearrange("p (h d) -> p h d", h=HEADS_PER_BLK),
+                in1=cos2[:, a, :].unsqueeze(1).to_broadcast([P, HEADS_PER_BLK, 128]),
+                op=MULT,
+            )
+            nc.vector.tensor_tensor(
+                out=crossed[:, i, :].rearrange("p (h j t) -> p h j t", h=HEADS_PER_BLK, t=2),
+                in0=acc[:].rearrange("p (h j t) -> p h j t", h=HEADS_PER_BLK, t=2)[:, :, :, ::-1],
+                in1=sin2[:, a, :].rearrange("p (j t) -> p j t", t=2).unsqueeze(1).to_broadcast([P, HEADS_PER_BLK, 64, 2]),
+                op=MULT,
+            )
+
         nc.gpsimd.memset(warm[:], 0.0)
         nc.vector.memset(xs[0][:].bitcast(I32), 0)
-        nc.vector.memset(ws[first_blk][:, 0:1, :].bitcast(I32), 0)
-        nc.vector.memset(ws[first_blk][:, 1:PASSES, :].bitcast(I32), 0)
-        load_codes(nc, wc[first_blk][:, 0:2, :], w_qkv_words, first_blk * N_BLK, N_BLK, 0, 2)
-        load_codes(nc, xc[0][:, 0:2, :], x_words, 0, CHUNK, 0, 2)
+        nc.vector.memset(ws[V_BLK][:, 0:1, :].bitcast(I32), 0)
+        nc.vector.memset(ws[V_BLK][:, 1:PASSES, :].bitcast(I32), 0)
+        load_codes(nc, wc[V_BLK], w_qkv_words, V_BLK * N_BLK, N_BLK, 0, 2)
+        load_codes(nc, xc[0], x_words, 0, CHUNK, 0, 2)
         load_scales(nc, xs[0], x_scales, 0, CHUNK)
-        load_scales_one_pass(nc, ws[first_blk], w_qkv_scales, first_blk * N_BLK, N_BLK, 0)
-        load_scales_one_pass(nc, ws[first_blk], w_qkv_scales, first_blk * N_BLK, N_BLK, 1)
-        load_codes(nc, wc[first_blk][:, 2:4, :], w_qkv_words, first_blk * N_BLK, N_BLK, 2, 4)
-        load_codes(nc, xc[0][:, 2:4, :], x_words, 0, CHUNK, 2, 4)
-        load_scales_one_pass(nc, ws[first_blk], w_qkv_scales, first_blk * N_BLK, N_BLK, 2)
-        load_scales_one_pass(nc, ws[first_blk], w_qkv_scales, first_blk * N_BLK, N_BLK, 3)
+        load_scales_one_pass(nc, ws[V_BLK], w_qkv_scales, V_BLK * N_BLK, N_BLK, 0)
+        load_scales_one_pass(nc, ws[V_BLK], w_qkv_scales, V_BLK * N_BLK, N_BLK, 1)
+        load_codes(nc, wc[V_BLK], w_qkv_words, V_BLK * N_BLK, N_BLK, 2, 4)
+        load_codes(nc, xc[0], x_words, 0, CHUNK, 2, 4)
+        load_scales_one_pass(nc, ws[V_BLK], w_qkv_scales, V_BLK * N_BLK, N_BLK, 2)
+        load_scales_one_pass(nc, ws[V_BLK], w_qkv_scales, V_BLK * N_BLK, N_BLK, 3)
         warm_acc = psum.tile([P, N_BLK], F32, name="acc")
         for w in range(N_WARM):
             nc.tensor.matmul(out=warm_acc[:], lhsT=warm[:, 0:P], rhs=warm[:, P : P + N_BLK], start=True, stop=True)
         for n in range(N_BLOCKS - 1):
             nc.vector.memset(ws[n][:].bitcast(I32), 0)
-            load_codes(nc, wc[n][:], w_qkv_words, n * N_BLK, N_BLK)
+            load_codes(nc, wc[n], w_qkv_words, n * N_BLK, N_BLK)
             load_scales(nc, ws[n], w_qkv_scales, n * N_BLK, N_BLK)
             if n == 0:
                 nc.sync.dma_start(out=cos_raw[:], in_=freqs_cos.rearrange("(a p) j -> p a j", p=P))
                 nc.sync.dma_start(out=sin_pm[:, 1], in_=freqs_sin.rearrange("(a p) j -> p a j", p=P))
         for s in range(1, N_CHUNKS):
             nc.vector.memset(xs[s][:].bitcast(I32), 0)
-        load_codes(nc, xc[1][:], x_words, CHUNK, CHUNK)
+        load_codes(nc, xc[1], x_words, CHUNK, CHUNK)
         load_scales(nc, xs[1], x_scales, CHUNK, CHUNK)
 
         nc.gpsimd.tensor_scalar(
@@ -121,87 +149,68 @@ def tile_causalselfattention_pa_kernel(
             in_=sin_pm[:].rearrange("p t a j -> p a j t"),
         )
 
-        for s in range(N_CHUNKS):
+        def value_block(s, dst):
             last = s == N_CHUNKS - 1
+            value = vals.tile([P, TILES_PER_CHUNK, N_BLK], F32, name="value")
+            accs = []
+            if s == 0:
+                for i in range(TILES_PER_CHUNK):
+                    acc = psum.tile([P, N_BLK], F32, name="acc")
+                    accs.append(acc)
+                for g in range(PASSES):
+                    for i in range(TILES_PER_CHUNK):
+                        mx_pass(accs[i], s, i, V_BLK, g)
+            for i in range(TILES_PER_CHUNK):
+                if s == 0:
+                    acc = accs[i]
+                else:
+                    acc = psum.tile([P, N_BLK], F32, name="acc")
+                    for g in range(PASSES):
+                        mx_pass(acc, s, i, V_BLK, g)
+                nc.scalar.copy(out=value[:, i, :], in_=acc[:])
+                if last:
+                    nc.scalar.dma_start(out=dst[:, i, :], in_=value[:, i, :])
+            if not last:
+                nc.scalar.dma_start(out=dst, in_=value[:])
+
+        def rope_block(s, n, dst):
+            last = s == N_CHUNKS - 1
+            direct = prod.tile([P, TILES_PER_CHUNK, N_BLK], F32, name="direct")
+            crossed = cross.tile([P, TILES_PER_CHUNK, N_BLK], F32, name="crossed")
+            for i in range(TILES_PER_CHUNK):
+                acc = psum.tile([P, N_BLK], F32, name="acc")
+                for g in range(PASSES):
+                    mx_pass(acc, s, i, n, g)
+                products(acc, direct, crossed, s, i)
+                if last and n < K_BLK and i % 2 == 1:
+                    half = slice(i - 1, i + 1)
+                    nc.gpsimd.tensor_tensor(out=direct[:, half, :], in0=direct[:, half, :], in1=crossed[:, half, :], op=ADD)
+                    nc.sync.dma_start(out=dst[:, half, :], in_=direct[:, half, :])
+            if last and n == K_BLK:
+                for i in range(TILES_PER_CHUNK):
+                    nc.vector.tensor_tensor(out=direct[:, i, :], in0=direct[:, i, :], in1=crossed[:, i, :], op=ADD)
+                    nc.sync.dma_start(out=dst[:, i, :], in_=direct[:, i, :])
+            elif not last:
+                nc.gpsimd.tensor_tensor(out=direct[:], in0=direct[:], in1=crossed[:], op=ADD)
+                nc.sync.dma_start(out=dst, in_=direct[:])
+
+        for s in range(N_CHUNKS):
             order = list(range(N_BLOCKS))
             if s == 0:
-                order = [first_blk] + order[:-1]
+                order = [V_BLK] + order[:-1]
             for n in order:
                 if n == order[3] and s + 2 < N_CHUNKS:
-                    load_codes(nc, xc[s + 2][:], x_words, (s + 2) * CHUNK, CHUNK)
+                    load_codes(nc, xc[s + 2], x_words, (s + 2) * CHUNK, CHUNK)
                     load_scales(nc, xs[s + 2], x_scales, (s + 2) * CHUNK, CHUNK)
-                rope = n < N_BLOCKS - 1
-                if n < 4:
-                    dst = q_rows[s * CHUNK : (s + 1) * CHUNK, n * N_BLK : (n + 1) * N_BLK]
-                elif n == 4:
-                    dst = k_rows[s * CHUNK : (s + 1) * CHUNK, :]
+                tokens = slice(s * CHUNK, (s + 1) * CHUNK)
+                if n < K_BLK:
+                    dst = q_rows[tokens, n * N_BLK : (n + 1) * N_BLK]
+                elif n == K_BLK:
+                    dst = k_rows[tokens, :]
                 else:
-                    dst = v_rows[s * CHUNK : (s + 1) * CHUNK, :]
+                    dst = v_rows[tokens, :]
                 dst = dst.rearrange("(i p) c -> p i c", p=P)
-                if rope:
-                    direct = prod.tile([P, TILES_PER_CHUNK, N_BLK], F32, name="direct")
-                    crossed = cross.tile([P, TILES_PER_CHUNK, N_BLK], F32, name="crossed")
+                if n == V_BLK:
+                    value_block(s, dst)
                 else:
-                    direct = vals.tile([P, TILES_PER_CHUNK, N_BLK], F32, name="value")
-                accs = []
-                if s == 0 and n == first_blk:
-                    for i in range(TILES_PER_CHUNK):
-                        acc = psum.tile([P, N_BLK], F32, name="acc")
-                        accs.append(acc)
-                    for g in range(PASSES):
-                        for i in range(TILES_PER_CHUNK):
-                            nc.tensor.matmul_mx(
-                                out=accs[i][:],
-                                lhsT=xc[s][:, g, 2 * TOK_TILE * i : 2 * TOK_TILE * (i + 1)].bitcast(FP4X4),
-                                lhsT_scale=xs[s][:, g, TOK_TILE * i : TOK_TILE * (i + 1)],
-                                rhs=wc[n][:, g, :].bitcast(FP4X4),
-                                rhs_scale=ws[n][:, g, :],
-                                start=(g == 0),
-                                stop=(g == PASSES - 1),
-                            )
-                for i in range(TILES_PER_CHUNK):
-                    if accs:
-                        acc = accs[i]
-                    else:
-                        acc = psum.tile([P, N_BLK], F32, name="acc")
-                    for g in range(PASSES if not accs else 0):
-                        nc.tensor.matmul_mx(
-                            out=acc[:],
-                            lhsT=xc[s][:, g, 2 * TOK_TILE * i : 2 * TOK_TILE * (i + 1)].bitcast(FP4X4),
-                            lhsT_scale=xs[s][:, g, TOK_TILE * i : TOK_TILE * (i + 1)],
-                            rhs=wc[n][:, g, :].bitcast(FP4X4),
-                            rhs_scale=ws[n][:, g, :],
-                            start=(g == 0),
-                            stop=(g == PASSES - 1),
-                        )
-                    if rope:
-                        a = (s * TILES_PER_CHUNK + i) % POS_TILES
-                        nc.vector.tensor_tensor(
-                            out=direct[:, i, :].rearrange("p (h d) -> p h d", h=HEADS_PER_BLK),
-                            in0=acc[:].rearrange("p (h d) -> p h d", h=HEADS_PER_BLK),
-                            in1=cos2[:, a, :].unsqueeze(1).to_broadcast([P, HEADS_PER_BLK, 128]),
-                            op=MULT,
-                        )
-                        nc.vector.tensor_tensor(
-                            out=crossed[:, i, :].rearrange("p (h j t) -> p h j t", h=HEADS_PER_BLK, t=2),
-                            in0=acc[:].rearrange("p (h j t) -> p h j t", h=HEADS_PER_BLK, t=2)[:, :, :, ::-1],
-                            in1=sin2[:, a, :].rearrange("p (j t) -> p j t", t=2).unsqueeze(1).to_broadcast([P, HEADS_PER_BLK, 64, 2]),
-                            op=MULT,
-                        )
-                        if last and n < 4 and i % 2 == 1:
-                            half = slice(i - 1, i + 1)
-                            nc.gpsimd.tensor_tensor(out=direct[:, half, :], in0=direct[:, half, :], in1=crossed[:, half, :], op=ADD)
-                            nc.sync.dma_start(out=dst[:, half, :], in_=direct[:, half, :])
-                    else:
-                        nc.scalar.copy(out=direct[:, i, :], in_=acc[:])
-                        if last:
-                            nc.scalar.dma_start(out=dst[:, i, :], in_=direct[:, i, :])
-                if rope and last and n == 4:
-                    for i in range(TILES_PER_CHUNK):
-                        nc.vector.tensor_tensor(out=direct[:, i, :], in0=direct[:, i, :], in1=crossed[:, i, :], op=ADD)
-                        nc.sync.dma_start(out=dst[:, i, :], in_=direct[:, i, :])
-                elif rope and not last:
-                    nc.gpsimd.tensor_tensor(out=direct[:], in0=direct[:], in1=crossed[:], op=ADD)
-                    nc.sync.dma_start(out=dst, in_=direct[:])
-                elif not last:
-                    nc.scalar.dma_start(out=dst, in_=direct[:])
+                    rope_block(s, n, dst)

@@ -24,7 +24,7 @@ V_BLK = N_BLOCKS - 1
 K_BLK = N_BLOCKS - 2
 POS_TILES = 1024 // TOK_TILE
 HEADS_PER_BLK = N_BLK // 128
-N_WARM = 6
+N_WARM = 10
 PERIOD = 28
 
 

@@ -26,6 +26,7 @@ POS_TILES = 1024 // TOK_TILE
 HEADS_PER_BLK = N_BLK // 128
 N_WARM = 10
 PERIOD = 28
+VALUE_AFTER = {1: 2, 2: 3, 3: 4, 4: 5, 6: 6, 7: 7}
 
 
 def load_codes(nc, tile, words, col0, ncols, g0=0, g1=PASSES):
@@ -111,15 +112,19 @@ def tile_causalselfattention_pa_kernel(
         nc.vector.memset(xs[0][:].bitcast(I32), 0)
         nc.vector.memset(ws[V_BLK][:, 0:1, :].bitcast(I32), 0)
         nc.vector.memset(ws[V_BLK][:, 1:PASSES, :].bitcast(I32), 0)
+        nc.vector.memset(xs[1][:].bitcast(I32), 0)
         load_codes(nc, wc[V_BLK], w_qkv_words, V_BLK * N_BLK, N_BLK, 0, 2)
         load_codes(nc, xc[0], x_words, 0, CHUNK, 0, 2)
         load_scales(nc, xs[0], x_scales, 0, CHUNK)
         load_scales_one_pass(nc, ws[V_BLK], w_qkv_scales, V_BLK * N_BLK, N_BLK, 0)
         load_scales_one_pass(nc, ws[V_BLK], w_qkv_scales, V_BLK * N_BLK, N_BLK, 1)
+        load_codes(nc, xc[1], x_words, CHUNK, CHUNK, 0, 2)
+        load_scales(nc, xs[1], x_scales, CHUNK, CHUNK)
         load_codes(nc, wc[V_BLK], w_qkv_words, V_BLK * N_BLK, N_BLK, 2, 4)
         load_codes(nc, xc[0], x_words, 0, CHUNK, 2, 4)
         load_scales_one_pass(nc, ws[V_BLK], w_qkv_scales, V_BLK * N_BLK, N_BLK, 2)
         load_scales_one_pass(nc, ws[V_BLK], w_qkv_scales, V_BLK * N_BLK, N_BLK, 3)
+        load_codes(nc, xc[1], x_words, CHUNK, CHUNK, 2, 4)
         warm_acc = psum.tile([P, N_BLK], F32, name="acc")
         for w in range(N_WARM):
             nc.tensor.matmul(out=warm_acc[:], lhsT=warm[:, 0:P], rhs=warm[:, P : P + N_BLK], start=True, stop=True)
@@ -130,10 +135,8 @@ def tile_causalselfattention_pa_kernel(
             if n == 0:
                 nc.sync.dma_start(out=cos_raw[:], in_=freqs_cos.rearrange("(a p) j -> p a j", p=P))
                 nc.sync.dma_start(out=sin_pm[:, 1], in_=freqs_sin.rearrange("(a p) j -> p a j", p=P))
-        for s in range(1, N_CHUNKS):
+        for s in range(2, N_CHUNKS):
             nc.vector.memset(xs[s][:].bitcast(I32), 0)
-        load_codes(nc, xc[1], x_words, CHUNK, CHUNK)
-        load_scales(nc, xs[1], x_scales, CHUNK, CHUNK)
 
         nc.gpsimd.tensor_scalar(
             out=cos2[:].rearrange("p a (j t) -> p a j t", t=2),
@@ -149,24 +152,40 @@ def tile_causalselfattention_pa_kernel(
             in_=sin_pm[:].rearrange("p t a j -> p a j t"),
         )
 
+        def out_rows(s, n):
+            tokens = slice(s * CHUNK, (s + 1) * CHUNK)
+            if n < K_BLK:
+                dst = q_rows[tokens, n * N_BLK : (n + 1) * N_BLK]
+            elif n == K_BLK:
+                dst = k_rows[tokens, :]
+            else:
+                dst = v_rows[tokens, :]
+            return dst.rearrange("(i p) c -> p i c", p=P)
+
+        def first_value_blocks():
+            accs = {}
+            for s in range(2):
+                for i in range(TILES_PER_CHUNK):
+                    acc = psum.tile([P, N_BLK], F32, name="acc")
+                    accs[(s, i)] = acc
+            for g0 in (0, 2):
+                for s in range(2):
+                    for g in (g0, g0 + 1):
+                        for i in range(TILES_PER_CHUNK):
+                            mx_pass(accs[(s, i)], s, i, V_BLK, g)
+            for s in range(2):
+                value = vals.tile([P, TILES_PER_CHUNK, N_BLK], F32, name="value")
+                for i in range(TILES_PER_CHUNK):
+                    nc.scalar.copy(out=value[:, i, :], in_=accs[(s, i)][:])
+                nc.scalar.dma_start(out=out_rows(s, V_BLK), in_=value[:])
+
         def value_block(s, dst):
             last = s == N_CHUNKS - 1
             value = vals.tile([P, TILES_PER_CHUNK, N_BLK], F32, name="value")
-            accs = []
-            if s == 0:
-                for i in range(TILES_PER_CHUNK):
-                    acc = psum.tile([P, N_BLK], F32, name="acc")
-                    accs.append(acc)
-                for g in range(PASSES):
-                    for i in range(TILES_PER_CHUNK):
-                        mx_pass(accs[i], s, i, V_BLK, g)
             for i in range(TILES_PER_CHUNK):
-                if s == 0:
-                    acc = accs[i]
-                else:
-                    acc = psum.tile([P, N_BLK], F32, name="acc")
-                    for g in range(PASSES):
-                        mx_pass(acc, s, i, V_BLK, g)
+                acc = psum.tile([P, N_BLK], F32, name="acc")
+                for g in range(PASSES):
+                    mx_pass(acc, s, i, V_BLK, g)
                 nc.scalar.copy(out=value[:, i, :], in_=acc[:])
                 if last:
                     nc.scalar.dma_start(out=dst[:, i, :], in_=value[:, i, :])
@@ -194,23 +213,12 @@ def tile_causalselfattention_pa_kernel(
                 nc.gpsimd.tensor_tensor(out=direct[:], in0=direct[:], in1=crossed[:], op=ADD)
                 nc.sync.dma_start(out=dst, in_=direct[:])
 
+        first_value_blocks()
         for s in range(N_CHUNKS):
-            order = list(range(N_BLOCKS))
-            if s == 0:
-                order = [V_BLK] + order[:-1]
-            for n in order:
-                if n == order[3] and s + 2 < N_CHUNKS:
+            for n in range(N_BLOCKS - 1):
+                if n == 3 and s + 2 < N_CHUNKS:
                     load_codes(nc, xc[s + 2], x_words, (s + 2) * CHUNK, CHUNK)
                     load_scales(nc, xs[s + 2], x_scales, (s + 2) * CHUNK, CHUNK)
-                tokens = slice(s * CHUNK, (s + 1) * CHUNK)
-                if n < K_BLK:
-                    dst = q_rows[tokens, n * N_BLK : (n + 1) * N_BLK]
-                elif n == K_BLK:
-                    dst = k_rows[tokens, :]
-                else:
-                    dst = v_rows[tokens, :]
-                dst = dst.rearrange("(i p) c -> p i c", p=P)
-                if n == V_BLK:
-                    value_block(s, dst)
-                else:
-                    rope_block(s, n, dst)
+                rope_block(s, n, out_rows(s, n))
+            if s in VALUE_AFTER:
+                value_block(VALUE_AFTER[s], out_rows(VALUE_AFTER[s], V_BLK))

@@ -108,9 +108,9 @@ def tile_causalselfattention_pa_kernel(
                 op=MULT,
             )
 
-        nc.gpsimd.memset(warm[:], 0.0)
         nc.vector.memset(xs[0][:].bitcast(I32), 0)
         nc.vector.memset(ws[V_BLK][:, 0:1, :].bitcast(I32), 0)
+        nc.vector.memset(warm[:], 0.0)
         nc.vector.memset(ws[V_BLK][:, 1:PASSES, :].bitcast(I32), 0)
         nc.vector.memset(xs[1][:].bitcast(I32), 0)
         load_codes(nc, wc[V_BLK], w_qkv_words, V_BLK * N_BLK, N_BLK, 0, 2)

@@ -25,7 +25,6 @@ K_BLK = N_BLOCKS - 2
 POS_TILES = 1024 // TOK_TILE
 HEADS_PER_BLK = N_BLK // 128
 N_WARM = 10
-PERIOD = 28
 VALUE_AFTER = {1: 2, 2: 3, 3: 4, 4: 5, 6: 6, 7: 7}
 
 
@@ -42,18 +41,6 @@ def load_scales(nc, plane, scales, col0, ncols):
             out=plane[r : P : 32, :, :].bitcast(I32),
             in_=scales[:, r : 16 : 4, col0 : col0 + ncols].rearrange("g q n -> q g n").bitcast(I32),
         )
-
-
-def load_scales_one_pass(nc, plane, scales, col0, ncols, g):
-    rows = scales.rearrange("g q n -> (g q) n")
-    repeats = [4, PERIOD, ncols // 4]
-    if g < PASSES - 1:
-        part = rows[16 * g : 16 * g + PERIOD, col0 : col0 + ncols].bitcast(I32)
-        nc.sync.dma_start(out=plane[0 : 4 * PERIOD, g, :].bitcast(I32), in_=part.unsqueeze(0).to_broadcast(repeats))
-    else:
-        part = rows[16 * g + 16 - PERIOD : 16 * g + 16, col0 : col0 + ncols].bitcast(I32)
-        nc.sync.dma_start(out=plane[16:P, g, :].bitcast(I32), in_=part.unsqueeze(0).to_broadcast(repeats))
-        nc.sync.dma_start(out=plane[0:16, g, :].bitcast(I32), in_=rows[16 * g : 16 * g + 16, col0 : col0 + ncols].bitcast(I32))
 
 
 def tile_causalselfattention_pa_kernel(
@@ -109,21 +96,19 @@ def tile_causalselfattention_pa_kernel(
             )
 
         nc.vector.memset(xs[0][:].bitcast(I32), 0)
-        nc.vector.memset(ws[V_BLK][:, 0:1, :].bitcast(I32), 0)
+        nc.vector.memset(ws[V_BLK][:].bitcast(I32), 0)
         nc.vector.memset(warm[:], 0.0)
-        nc.vector.memset(ws[V_BLK][:, 1:PASSES, :].bitcast(I32), 0)
         nc.vector.memset(xs[1][:].bitcast(I32), 0)
-        load_codes(nc, wc[V_BLK], w_qkv_words, V_BLK * N_BLK, N_BLK, 0, 2)
-        load_codes(nc, xc[0], x_words, 0, CHUNK, 0, 2)
+        load_codes(nc, wc[V_BLK], w_qkv_words, V_BLK * N_BLK, N_BLK, 0, 1)
+        load_codes(nc, xc[0], x_words, 0, CHUNK, 0, 1)
         load_scales(nc, xs[0], x_scales, 0, CHUNK)
-        load_scales_one_pass(nc, ws[V_BLK], w_qkv_scales, V_BLK * N_BLK, N_BLK, 0)
-        load_scales_one_pass(nc, ws[V_BLK], w_qkv_scales, V_BLK * N_BLK, N_BLK, 1)
+        load_scales(nc, ws[V_BLK], w_qkv_scales, V_BLK * N_BLK, N_BLK)
+        load_codes(nc, wc[V_BLK], w_qkv_words, V_BLK * N_BLK, N_BLK, 1, 2)
+        load_codes(nc, xc[0], x_words, 0, CHUNK, 1, 2)
         load_codes(nc, xc[1], x_words, CHUNK, CHUNK, 0, 2)
         load_scales(nc, xs[1], x_scales, CHUNK, CHUNK)
         load_codes(nc, wc[V_BLK], w_qkv_words, V_BLK * N_BLK, N_BLK, 2, 4)
         load_codes(nc, xc[0], x_words, 0, CHUNK, 2, 4)
-        load_scales_one_pass(nc, ws[V_BLK], w_qkv_scales, V_BLK * N_BLK, N_BLK, 2)
-        load_scales_one_pass(nc, ws[V_BLK], w_qkv_scales, V_BLK * N_BLK, N_BLK, 3)
         load_codes(nc, xc[1], x_words, CHUNK, CHUNK, 2, 4)
         warm_acc = psum.tile([P, N_BLK], F32, name="acc")
         for w in range(N_WARM):

@@ -24,7 +24,7 @@ V_BLK = N_BLOCKS - 1
 K_BLK = N_BLOCKS - 2
 POS_TILES = 1024 // TOK_TILE
 HEADS_PER_BLK = N_BLK // 128
-N_WARM = 10
+N_WARM = 7
 VALUE_AFTER = {1: 2, 2: 3, 3: 4, 4: 5, 6: 6, 7: 7}
 
 
@@ -95,9 +95,9 @@ def tile_causalselfattention_pa_kernel(
                 op=MULT,
             )
 
+        nc.vector.memset(warm[:], 0.0)
         nc.vector.memset(xs[0][:].bitcast(I32), 0)
         nc.vector.memset(ws[V_BLK][:].bitcast(I32), 0)
-        nc.vector.memset(warm[:], 0.0)
         nc.vector.memset(xs[1][:].bitcast(I32), 0)
         load_codes(nc, wc[V_BLK], w_qkv_words, V_BLK * N_BLK, N_BLK, 0, 1)
         load_codes(nc, xc[0], x_words, 0, CHUNK, 0, 1)

@@ -25,7 +25,7 @@ K_BLK = N_BLOCKS - 2
 POS_TILES = 1024 // TOK_TILE
 HEADS_PER_BLK = N_BLK // 128
 N_WARM = 7
-VALUE_AFTER = {1: 2, 2: 3, 3: 4, 4: 5, 6: 6, 7: 7}
+VALUE_AFTER = {7: 2, 14: 3, 21: 4, 28: 5, 36: 6, 39: 7}
 
 
 def load_codes(nc, tile, words, col0, ncols, g0=0, g1=PASSES):
@@ -205,5 +205,6 @@ def tile_causalselfattention_pa_kernel(
                     load_codes(nc, xc[s + 2], x_words, (s + 2) * CHUNK, CHUNK)
                     load_scales(nc, xs[s + 2], x_scales, (s + 2) * CHUNK, CHUNK)
                 rope_block(s, n, out_rows(s, n))
-            if s in VALUE_AFTER:
-                value_block(VALUE_AFTER[s], out_rows(VALUE_AFTER[s], V_BLK))
+                done = (N_BLOCKS - 1) * s + n
+                if done in VALUE_AFTER:
+                    value_block(VALUE_AFTER[done], out_rows(VALUE_AFTER[done], V_BLK))

@@ -25,7 +25,7 @@ K_BLK = N_BLOCKS - 2
 POS_TILES = 1024 // TOK_TILE
 HEADS_PER_BLK = N_BLK // 128
 N_WARM = 7
-VALUE_AFTER = {7: 2, 14: 3, 21: 4, 28: 5, 36: 6, 39: 7}
+VALUE_AFTER = {7: 2, 15: 3, 22: 4, 30: 5, 37: 6, 39: 7}
 
 
 def load_codes(nc, tile, words, col0, ncols, g0=0, g1=PASSES):

from contextlib import ExitStack

import concourse.mybir as mybir

FLOPS = 2 * 4096 * 2048 * 3072

F32 = mybir.dt.float32
BF16 = mybir.dt.bfloat16
I32 = mybir.dt.int32
U8 = mybir.dt.uint8
FP4X4 = mybir.dt.float4_e2m1fn_x4
MULT = mybir.AluOpType.mult
ADD = mybir.AluOpType.add

P = 128
PASSES = 4
TOK_TILE = 128
N_BLK = 512
TILES_PER_CHUNK = 4
CHUNK = TOK_TILE * TILES_PER_CHUNK
N_CHUNKS = 4096 // CHUNK
N_BLOCKS = 3072 // N_BLK
V_BLK = N_BLOCKS - 1
K_BLK = N_BLOCKS - 2
POS_TILES = 1024 // TOK_TILE
HEADS_PER_BLK = N_BLK // 128
N_WARM = 7
VALUE_AFTER = {7: 2, 15: 3, 22: 4, 30: 5, 37: 6, 39: 7}


def load_codes(nc, tile, words, col0, ncols, g0=0, g1=PASSES):
    nc.sync.dma_start(
        out=tile[:, g0:g1, :].bitcast(I32),
        in_=words[g0:g1, :, 2 * col0 : 2 * (col0 + ncols)].rearrange("g p b -> p g b").bitcast(I32),
    )


def load_scales(nc, plane, scales, col0, ncols):
    for r in range(4):
        nc.sync.dma_start(
            out=plane[r : P : 32, :, :].bitcast(I32),
            in_=scales[:, r : 16 : 4, col0 : col0 + ncols].rearrange("g q n -> q g n").bitcast(I32),
        )


def tile_causalselfattention_pa_kernel(
    tc, x_words, x_scales, w_qkv_words, w_qkv_scales, freqs_cos, freqs_sin, out_0, out_1, out_2
):
    nc = tc.nc
    q_rows = out_0.rearrange("b t h d -> (b t) (h d)")
    k_rows = out_1.rearrange("b t h d -> (b t) (h d)")
    v_rows = out_2.rearrange("b t h d -> (b t) (h d)")

    with ExitStack() as ctx:
        keep = ctx.enter_context(tc.tile_pool(name="keep", bufs=1))
        prod = ctx.enter_context(tc.tile_pool(name="prod", bufs=8))
        cross = ctx.enter_context(tc.tile_pool(name="cross", bufs=3))
        vals = ctx.enter_context(tc.tile_pool(name="vals", bufs=3))
        psum = ctx.enter_context(tc.psum_pool(name="psum", bufs=8))
        ctx.enter_context(tc.manual_schedule())

        xc = [keep.tile([P, PASSES, 2 * CHUNK], U8, name="xc%d" % s, align_bytes=256) for s in range(N_CHUNKS)]
        xs = [keep.tile([P, PASSES, CHUNK], U8, name="xs%d" % s, align_bytes=256) for s in range(N_CHUNKS)]
        wc = [keep.tile([P, PASSES, 2 * N_BLK], U8, name="wc%d" % n, align_bytes=256) for n in range(N_BLOCKS)]
        ws = [keep.tile([P, PASSES, N_BLK], U8, name="ws%d" % n, align_bytes=256) for n in range(N_BLOCKS)]
        cos_raw = keep.tile([P, POS_TILES, 64], BF16, name="cos_raw")
        sin_pm = keep.tile([P, 2, POS_TILES, 64], BF16, name="sin_pm")
        cos2 = keep.tile([P, POS_TILES, 128], F32, name="cos2")
        sin2 = keep.tile([P, POS_TILES, 128], F32, name="sin2")
        warm = keep.tile([P, P + N_BLK], BF16, name="warm")

        def mx_pass(acc, s, i, n, g, c0=0, c1=N_BLK):
            nc.tensor.matmul_mx(
                out=acc[:],
                lhsT=xc[s][:, g, 2 * TOK_TILE * i : 2 * TOK_TILE * (i + 1)].bitcast(FP4X4),
                lhsT_scale=xs[s][:, g, TOK_TILE * i : TOK_TILE * (i + 1)],
                rhs=wc[n][:, g, 2 * c0 : 2 * c1].bitcast(FP4X4),
                rhs_scale=ws[n][:, g, c0:c1],
                start=(g == 0),
                stop=(g == PASSES - 1),
            )

        def products(acc, direct, crossed, s, i):
            a = (s * TILES_PER_CHUNK + i) % POS_TILES
            nc.vector.tensor_tensor(
                out=direct[:, i, :].rearrange("p (h d) -> p h d", h=HEADS_PER_BLK),
                in0=acc[:].rearrange("p (h d) -> p h d", h=HEADS_PER_BLK),
                in1=cos2[:, a, :].unsqueeze(1).to_broadcast([P, HEADS_PER_BLK, 128]),
                op=MULT,
            )
            nc.vector.tensor_tensor(
                out=crossed[:, i, :].rearrange("p (h j t) -> p h j t", h=HEADS_PER_BLK, t=2),
                in0=acc[:].rearrange("p (h j t) -> p h j t", h=HEADS_PER_BLK, t=2)[:, :, :, ::-1],
                in1=sin2[:, a, :].rearrange("p (j t) -> p j t", t=2).unsqueeze(1).to_broadcast([P, HEADS_PER_BLK, 64, 2]),
                op=MULT,
            )

        nc.vector.memset(warm[:], 0.0)
        nc.vector.memset(xs[0][:].bitcast(I32), 0)
        nc.vector.memset(ws[V_BLK][:].bitcast(I32), 0)
        nc.vector.memset(xs[1][:].bitcast(I32), 0)
        load_codes(nc, wc[V_BLK], w_qkv_words, V_BLK * N_BLK, N_BLK, 0, 1)
        load_codes(nc, xc[0], x_words, 0, CHUNK, 0, 1)
        load_scales(nc, xs[0], x_scales, 0, CHUNK)
        load_scales(nc, ws[V_BLK], w_qkv_scales, V_BLK * N_BLK, N_BLK)
        load_codes(nc, wc[V_BLK], w_qkv_words, V_BLK * N_BLK, N_BLK, 1, 2)
        load_codes(nc, xc[0], x_words, 0, CHUNK, 1, 2)
        load_codes(nc, xc[1], x_words, CHUNK, CHUNK, 0, 2)
        load_scales(nc, xs[1], x_scales, CHUNK, CHUNK)
        load_codes(nc, wc[V_BLK], w_qkv_words, V_BLK * N_BLK, N_BLK, 2, 4)
        load_codes(nc, xc[0], x_words, 0, CHUNK, 2, 4)
        load_codes(nc, xc[1], x_words, CHUNK, CHUNK, 2, 4)
        warm_acc = psum.tile([P, N_BLK], F32, name="acc")
        for w in range(N_WARM):
            nc.tensor.matmul(out=warm_acc[:], lhsT=warm[:, 0:P], rhs=warm[:, P : P + N_BLK], start=True, stop=True)
        for n in range(N_BLOCKS - 1):
            nc.vector.memset(ws[n][:].bitcast(I32), 0)
            load_codes(nc, wc[n], w_qkv_words, n * N_BLK, N_BLK)
            load_scales(nc, ws[n], w_qkv_scales, n * N_BLK, N_BLK)
            if n == 0:
                nc.sync.dma_start(out=cos_raw[:], in_=freqs_cos.rearrange("(a p) j -> p a j", p=P))
                nc.sync.dma_start(out=sin_pm[:, 1], in_=freqs_sin.rearrange("(a p) j -> p a j", p=P))
        for s in range(2, N_CHUNKS):
            nc.vector.memset(xs[s][:].bitcast(I32), 0)

        nc.gpsimd.tensor_scalar(
            out=cos2[:].rearrange("p a (j t) -> p a j t", t=2),
            in0=cos_raw[:].unsqueeze(3).to_broadcast([P, POS_TILES, 64, 2]),
            scalar1=1.0,
            scalar2=0.0,
            op0=MULT,
            op1=ADD,
        )
        nc.vector.tensor_scalar_mul(out=sin_pm[:, 0], in0=sin_pm[:, 1], scalar1=-1.0)
        nc.vector.tensor_copy(
            out=sin2[:].rearrange("p a (j t) -> p a j t", t=2),
            in_=sin_pm[:].rearrange("p t a j -> p a j t"),
        )

        def out_rows(s, n):
            tokens = slice(s * CHUNK, (s + 1) * CHUNK)
            if n < K_BLK:
                dst = q_rows[tokens, n * N_BLK : (n + 1) * N_BLK]
            elif n == K_BLK:
                dst = k_rows[tokens, :]
            else:
                dst = v_rows[tokens, :]
            return dst.rearrange("(i p) c -> p i c", p=P)

        def first_value_blocks():
            accs = {}
            for s in range(2):
                for i in range(TILES_PER_CHUNK):
                    acc = psum.tile([P, N_BLK], F32, name="acc")
                    accs[(s, i)] = acc
            for g0 in (0, 2):
                for s in range(2):
                    for g in (g0, g0 + 1):
                        for i in range(TILES_PER_CHUNK):
                            mx_pass(accs[(s, i)], s, i, V_BLK, g)
            for s in range(2):
                value = vals.tile([P, TILES_PER_CHUNK, N_BLK], F32, name="value")
                for i in range(TILES_PER_CHUNK):
                    nc.scalar.copy(out=value[:, i, :], in_=accs[(s, i)][:])
                nc.scalar.dma_start(out=out_rows(s, V_BLK), in_=value[:])

        def value_block(s, dst):
            last = s == N_CHUNKS - 1
            value = vals.tile([P, TILES_PER_CHUNK, N_BLK], F32, name="value")
            for i in range(TILES_PER_CHUNK):
                acc = psum.tile([P, N_BLK], F32, name="acc")
                for g in range(PASSES):
                    mx_pass(acc, s, i, V_BLK, g)
                nc.scalar.copy(out=value[:, i, :], in_=acc[:])
                if last:
                    nc.scalar.dma_start(out=dst[:, i, :], in_=value[:, i, :])
            if not last:
                nc.scalar.dma_start(out=dst, in_=value[:])

        def rope_block(s, n, dst):
            last = s == N_CHUNKS - 1
            direct = prod.tile([P, TILES_PER_CHUNK, N_BLK], F32, name="direct")
            crossed = cross.tile([P, TILES_PER_CHUNK, N_BLK], F32, name="crossed")
            for i in range(TILES_PER_CHUNK):
                acc = psum.tile([P, N_BLK], F32, name="acc")
                for g in range(PASSES):
                    mx_pass(acc, s, i, n, g)
                products(acc, direct, crossed, s, i)
                if last and n < K_BLK and i % 2 == 1:
                    half = slice(i - 1, i + 1)
                    nc.gpsimd.tensor_tensor(out=direct[:, half, :], in0=direct[:, half, :], in1=crossed[:, half, :], op=ADD)
                    nc.sync.dma_start(out=dst[:, half, :], in_=direct[:, half, :])
            if last and n == K_BLK:
                for i in range(TILES_PER_CHUNK):
                    nc.vector.tensor_tensor(out=direct[:, i, :], in0=direct[:, i, :], in1=crossed[:, i, :], op=ADD)
                    nc.sync.dma_start(out=dst[:, i, :], in_=direct[:, i, :])
            elif not last:
                nc.gpsimd.tensor_tensor(out=direct[:], in0=direct[:], in1=crossed[:], op=ADD)
                nc.sync.dma_start(out=dst, in_=direct[:])

        first_value_blocks()
        for s in range(N_CHUNKS):
            for n in range(N_BLOCKS - 1):
                if n == 3 and s + 2 < N_CHUNKS:
                    load_codes(nc, xc[s + 2], x_words, (s + 2) * CHUNK, CHUNK)
                    load_scales(nc, xs[s + 2], x_scales, (s + 2) * CHUNK, CHUNK)
                rope_block(s, n, out_rows(s, n))
                done = (N_BLOCKS - 1) * s + n
                if done in VALUE_AFTER:
                    value_block(VALUE_AFTER[done], out_rows(VALUE_AFTER[done], V_BLK))
